import numpy as np
import ml_dtypes


def mxq(x, axis, fmt="e4m3"):
    dtype, down = {"e4m3": (ml_dtypes.float8_e4m3fn, 7), "e5m2": (ml_dtypes.float8_e5m2, 14)}[fmt]
    v = np.moveaxis(np.asarray(x, np.float32).astype(ml_dtypes.bfloat16).astype(np.float64), axis, -1)
    blocks = v.reshape(v.shape[:-1] + (-1, 32))
    amax = np.abs(blocks).max(-1, keepdims=True)
    byte = np.maximum(np.where(amax > 0, np.frexp(amax)[1] - 1 + 127, 0) - down, 1)
    scale = np.exp2(byte - 127.0)
    codes = (blocks / scale).astype(np.float32).astype(dtype).astype(np.float64)
    return np.moveaxis((codes * scale).reshape(v.shape), -1, axis)


WIDE = False


def mx_kscale(k):
    if not WIDE:
        return np.ones(k)
    levels = np.array([10, -10, 5, -5, 0])
    if k % 512:
        return np.exp2(np.random.permutation(np.resize(levels, k // 32))).repeat(32)
    a = np.empty((k // 512, 16))
    for p in range(k // 512):
        a[p, :8] = np.random.permutation(np.resize(levels, 8))
        for g in range(8):
            far = levels[np.abs(levels - a[p, g]) >= 10]
            a[p, g + 8] = far[np.random.randint(len(far))]
    return np.exp2(a.ravel()).repeat(32)


BF16 = ml_dtypes.bfloat16


def bf(x):
    return np.asarray(x, np.float32).astype(BF16)


def f64(x):
    return np.asarray(x).astype(np.float64)


B, N, D, F, H = 1, 1024, 1024, 1024, 16
DH = F // H
EPS = 1e-12


def l2norm(t):
    nrm = np.sqrt(np.sum(t * t, axis=-1, keepdims=True))
    return t / np.maximum(nrm, EPS)


def draw0():
    s = mx_kscale(D)
    return {"x": bf(np.random.standard_normal((B, N, D)) * s),
            "Wq": bf(np.random.standard_normal((D, F)) / np.sqrt(D) / s[:, None]),
            "Wk": bf(np.random.standard_normal((D, F)) / np.sqrt(D) / s[:, None])}


def core(x, Wq, Wk):
    xq = mxq(f64(x), 2, "e4m3")

    def heads(W):
        y = xq @ mxq(f64(W), 0, "e4m3")
        return y.reshape(B, N, H, DH).transpose(0, 2, 1, 3)

    return l2norm(heads(Wq)), l2norm(heads(Wk))


def e4m3fn_bytes(y):
    return np.clip(np.asarray(y, np.float64), -448.0, 448.0).astype(np.float32).astype(ml_dtypes.float8_e4m3fn).view(np.uint8)


def e4m3fn_values(b):
    return np.asarray(b, np.uint8).view(ml_dtypes.float8_e4m3fn).astype(np.float64)


def setup_inputs():
    d = draw0()
    x0 = np.asarray(d['x']).astype(np.float64)
    s = (np.max(np.abs(x0), axis=(0, 1), keepdims=True) / 448.0).astype(np.float32)
    out = {}
    for k, v in d.items():
        if k == 'x':
            out['x_bytes'] = e4m3fn_bytes(x0 / s.astype(np.float64))
            out['x_scale'] = s
        else:
            out[k] = v
    return out


def reference(x_bytes, x_scale, Wq, Wk):
    return core(e4m3fn_values(x_bytes) * x_scale.astype(np.float64), Wq, Wk)

@@ -1,0 +1,214 @@
+from contextlib import ExitStack
+
+import concourse.mybir as mybir
+from concourse.masks import make_identity
+
+FLOPS = 2 * 1024 * 1024 * 2048
+
+F32 = mybir.dt.float32
+BF16 = mybir.dt.bfloat16
+U8 = mybir.dt.uint8
+U32 = mybir.dt.uint32
+FP8 = mybir.dt.float8_e4m3fn
+FP8X4 = mybir.dt.float8_e4m3fn_x4
+ACT = mybir.ActivationFunctionType
+ALU = mybir.AluOpType
+
+P = 128
+NJ = 8
+K = 1024
+NG = 2
+NC = 4
+CW = 512
+HD = 64
+HPG = 8
+
+MANUAL = False
+WI_ENGINE = {(0, 0): "s", (0, 1): "v", (1, 0): "s", (1, 1): "v",
+             (2, 0): "g", (2, 1): "g", (3, 0): "g", (3, 1): "g"}
+WI_PIECES = 2
+STORE_RUNS = {0: (4, 4), 1: (4, 4), 2: (4, 4), 3: (4, 2, 1, 1)}
+
+
+def tile_attention_pa_kernel(tc, x_bytes, x_scale, Wq, Wk, out_0, out_1):
+    nc = tc.nc
+    with ExitStack() as ctx:
+        if MANUAL:
+            ctx.enter_context(tc.manual_schedule())
+        keep = ctx.enter_context(tc.tile_pool(name="keep", bufs=1))
+        small = ctx.enter_context(tc.tile_pool(name="small", bufs=6))
+        shared = ctx.enter_context(tc.tile_pool(name="shared", bufs=1))
+        psum_t = ctx.enter_context(tc.psum_pool(name="psum_t", bufs=2))
+        psum_y = ctx.enter_context(tc.psum_pool(name="psum_y", bufs=6))
+
+        xv = x_bytes.rearrange("o (p j) k -> p (o j) k", j=NJ)
+        wviews = [w.rearrange("(g p t) n -> g p t n", g=NG, t=4) for w in (Wq, Wk)]
+        oviews = [o.rearrange("o h (p j) d -> p (o h) j d", j=NJ) for o in (out_0, out_1)]
+
+        xbytes = [keep.tile([P, 2, K], U8, name="xbytes%d" % i) for i in range(NJ // 2)]
+        xs = keep.tile([P, K], F32, name="xs")
+        wraw = {}
+        for c in range(NC):
+            for g in range(NG):
+                wraw[(c, g)] = keep.tile([P, 4, CW], BF16, name="wraw%d_%d" % (c, g))
+
+        def load_x(i):
+            nc.sync.dma_start(out=xbytes[i][:], in_=xv[:, 2 * i:2 * i + 2, :])
+
+        def load_w(c, g):
+            n0 = (c % 2) * CW
+            nc.sync.dma_start(out=wraw[(c, g)][:], in_=wviews[c // 2][g, :, :, n0:n0 + CW])
+
+        nc.scalar.dma_start(out=xs[:], in_=x_scale.rearrange("a b k -> (a b k)").partition_broadcast(P))
+        load_x(0)
+        load_w(0, 0)
+        load_w(0, 1)
+        load_x(1)
+        load_w(1, 0)
+        load_w(1, 1)
+        load_x(2)
+        load_x(3)
+        for c in range(2, NC):
+            for g in range(NG):
+                load_w(c, g)
+
+        ident = keep.tile([P, P], F32, name="ident")
+        make_identity(nc, ident[:])
+
+        warm = keep.tile([P, 1], F32, name="warm")
+        nc.vector.memset(warm[:], 1.0)
+        warm2 = keep.tile([P, 1], F32, name="warm2")
+        nc.scalar.activation(out=warm2[:], in_=warm[:], func=ACT.Abs_reciprocal_sqrt)
+
+        xb, xg, xc, xsc = {}, {}, {}, {}
+
+        def product(j):
+            xb[j] = keep.tile([P, K], BF16, name="xb%d" % j)
+            nc.vector.tensor_tensor(out=xb[j][:], in0=xbytes[j // 2][:, j % 2, :].bitcast(FP8), in1=xs[:], op=ALU.mult)
+
+        def turn(j):
+            words = xb[j][:].bitcast(F32)
+            pt = psum_t.tile([P, NG, 2, P], F32, name="pt")
+            for g in range(NG):
+                for u in range(2):
+                    nc.tensor.transpose(pt[:, g, u, :], words[:, 256 * g + u:256 * (g + 1):2], ident[:])
+            if j < 4:
+                xg[j] = keep.tile([P, NG * P * 4], BF16, name="xg%d" % j, align_bytes=64)
+            else:
+                xg[j] = shared.tile([P, NG * P * 4], BF16, name="xg%d" % j, align_bytes=64, offset=(j - 4) * 2048)
+            nc.scalar.copy(
+                out=xg[j][:].bitcast(F32).rearrange("p (g r u) -> p g r u", g=NG, u=2),
+                in_=pt[:].rearrange("p g u r -> p g r u"),
+            )
+
+        def quant_x(j):
+            xc[j] = keep.tile([P, NG * P], U32, name="xc%d" % j, align_bytes=64)
+            xsc[j] = keep.tile([P, NG * P], U8, name="xsc%d" % j, align_bytes=64)
+            nc.vector.quantize_mx(out=xc[j][:].bitcast(FP8X4), scales=xsc[j][:], in_=xg[j][:])
+
+        wg, wc, wsc = {}, {}, {}
+
+        def interleave_w(c, g, piece):
+            if c not in wg:
+                if c == 2:
+                    wg[c] = shared.tile([P, NG, CW, 4], BF16, name="wg%d" % c, align_bytes=64, offset=0)
+                else:
+                    wg[c] = keep.tile([P, NG, CW, 4], BF16, name="wg%d" % c, align_bytes=64)
+            w = CW // WI_PIECES
+            a = piece * w
+            dst = wg[c][:, g, a:a + w, :]
+            src = wraw[(c, g)][:, :, a:a + w].rearrange("p t n -> p n t")
+            e = WI_ENGINE[(c, g)]
+            if e == "v":
+                nc.vector.tensor_copy(out=dst, in_=src)
+            elif e == "s":
+                nc.scalar.copy(out=dst, in_=src)
+            else:
+                nc.gpsimd.tensor_scalar(out=dst, in0=src, scalar1=1.0, scalar2=0.0, op0=ALU.mult, op1=ALU.add)
+
+        def quant_w(c):
+            wc[c] = keep.tile([P, NG * CW], U32, name="wc%d" % c, align_bytes=64)
+            wsc[c] = keep.tile([P, NG * CW], U8, name="wsc%d" % c, align_bytes=64)
+            nc.vector.quantize_mx(out=wc[c][:].bitcast(FP8X4), scales=wsc[c][:],
+                                  in_=wg[c][:].rearrange("p g n t -> p (g n t)"))
+
+        bank, rn, res = {}, {}, {}
+
+        def multiply(c, j):
+            acc = psum_y.tile([P, CW], F32, name="acc")
+            bank[(c, j)] = acc
+            for g in range(NG):
+                nc.tensor.matmul_mx(
+                    out=acc[:],
+                    lhsT=xc[j][:, P * g:P * (g + 1)].bitcast(FP8X4),
+                    lhsT_scale=xsc[j][:, P * g:P * (g + 1)],
+                    rhs=wc[c][:, CW * g:CW * (g + 1)].bitcast(FP8X4),
+                    rhs_scale=wsc[c][:, CW * g:CW * (g + 1)],
+                    start=(g == 0),
+                    stop=(g == NG - 1),
+                )
+
+        def norms(c, j):
+            acc = bank[(c, j)]
+            ss = small.tile([P, HPG], F32, name="ss")
+            junk = small.tile([P, CW], BF16, name="junk")
+            for h in range(HPG):
+                nc.scalar.activation(out=junk[:, HD * h:HD * (h + 1)], in_=acc[:, HD * h:HD * (h + 1)], func=ACT.Square,
+                                     accum_out=ss[:, h:h + 1])
+            r = small.tile([P, HPG], F32, name="rn")
+            nc.scalar.activation(out=r[:], in_=ss[:], func=ACT.Abs_reciprocal_sqrt)
+            rn[(c, j)] = r
+
+        def scale_out(c, j):
+            j0 = 0
+            for jw in STORE_RUNS[c]:
+                if j < j0 + jw:
+                    break
+                j0 += jw
+            if (c, j0) not in res:
+                res[(c, j0)] = keep.tile([P, HPG, jw, HD], F32, name="res%d_%d" % (c, j0))
+            nc.vector.scalar_tensor_tensor(
+                out=res[(c, j0)][:, :, j - j0, :],
+                in0=rn[(c, j)][:].unsqueeze(2).to_broadcast([P, HPG, HD]),
+                scalar=1.0e12,
+                in1=bank[(c, j)][:].rearrange("p (h d) -> p h d", d=HD),
+                op0=ALU.min,
+                op1=ALU.mult,
+            )
+            if j == j0 + jw - 1:
+                h0 = (c % 2) * HPG
+                nc.sync.dma_start(out=oviews[c // 2][:, h0:h0 + HPG, j0:j0 + jw, :], in_=res[(c, j0)][:])
+
+        product(0)
+        turn(0)
+        product(1)
+        turn(1)
+        for piece in range(WI_PIECES):
+            interleave_w(0, 0, piece)
+            interleave_w(0, 1, piece)
+        quant_w(0)
+        quant_x(0)
+        product(2)
+        banks = [(c, j) for c in range(NC) for j in range(NJ)]
+        for i, (c, j) in enumerate(banks):
+            if i + 3 < NJ:
+                product(i + 3)
+            if i + 2 < NJ:
+                turn(i + 2)
+            if i + 1 < NJ:
+                quant_x(i + 1)
+            multiply(c, j)
+            norms(c, j)
+            if i >= 1:
+                scale_out(*banks[i - 1])
+            if i in (1, 2):
+                interleave_w(1, 0, i - 1)
+                interleave_w(1, 1, i - 1)
+            if i == 7:
+                for cc in (2, 3):
+                    for g in range(NG):
+                        for piece in range(WI_PIECES):
+                            interleave_w(cc, g, piece)
+            if c + 1 < NC and j == 4:
+                quant_w(c + 1)
+        scale_out(*banks[-1])

@@ -1,3 +1,4 @@
+import math
 from contextlib import ExitStack
 
 import concourse.mybir as mybir
@@ -13,6 +14,7 @@ FP8 = mybir.dt.float8_e4m3fn
 FP8X4 = mybir.dt.float8_e4m3fn_x4
 ACT = mybir.ActivationFunctionType
 ALU = mybir.AluOpType
+AX = mybir.AxisListType
 
 P = 128
 NJ = 8
@@ -28,6 +30,11 @@ WI_ENGINE = {(0, 0): "s", (0, 1): "v", (1, 0): "s", (1, 1): "v",
              (2, 0): "g", (2, 1): "g", (3, 0): "g", (3, 1): "g"}
 WI_PIECES = 2
 STORE_RUNS = {0: (4, 4), 1: (4, 4), 2: (4, 4), 3: (4, 2, 1, 1)}
+V_TILES = (0, 3, 6)
+
+
+def by_vector(c, j):
+    return c >= 1 and j in V_TILES
 
 
 def tile_attention_pa_kernel(tc, x_bytes, x_scale, Wq, Wk, out_0, out_1):
@@ -148,16 +155,34 @@ def tile_attention_pa_kernel(tc, x_bytes, x_scale, Wq, Wk, out_0, out_1):
                     stop=(g == NG - 1),
                 )
 
-        def norms(c, j):
+        stats = {}
+
+        def sums_vector(c, j):
             acc = bank[(c, j)]
-            ss = small.tile([P, HPG], F32, name="ss")
+            st = small.tile([P, HPG, 2, 3], F32, name="st")
+            for h in range(HPG):
+                nc.vector.bn_stats(out=st[:, h, :, :].rearrange("p e s -> p (e s)"), in_=acc[:, HD * h:HD * (h + 1)])
+            stats[(c, j)] = st
+
+        def sums_scalar(c, j):
+            acc = bank[(c, j)]
+            before = (c, j - 1) if by_vector(c, j - 1) else None
+            ss = small.tile([P, 2, HPG], F32, name="ss")
             junk = small.tile([P, CW], BF16, name="junk")
             for h in range(HPG):
                 nc.scalar.activation(out=junk[:, HD * h:HD * (h + 1)], in_=acc[:, HD * h:HD * (h + 1)], func=ACT.Square,
-                                     accum_out=ss[:, h:h + 1])
-            r = small.tile([P, HPG], F32, name="rn")
-            nc.scalar.activation(out=r[:], in_=ss[:], func=ACT.Abs_reciprocal_sqrt)
-            rn[(c, j)] = r
+                                     accum_out=ss[:, 1, h:h + 1])
+                if h == 4 and before is not None:
+                    means = stats[before][:, :, :, 1:2]
+                    nc.scalar.activation(out=means, in_=means, func=ACT.Square, scale=math.sqrt(HD / 2))
+            r = small.tile([P, 2, HPG], F32, name="rn")
+            if before is not None:
+                nc.vector.tensor_reduce(out=ss[:, 0, :], in_=stats[before][:, :, :, 1:3], axis=AX.XY, op=ALU.add)
+                nc.scalar.activation(out=r[:], in_=ss[:], func=ACT.Abs_reciprocal_sqrt)
+                rn[before] = r[:, 0, :]
+            else:
+                nc.scalar.activation(out=r[:, 1, :], in_=ss[:, 1, :], func=ACT.Abs_reciprocal_sqrt)
+            rn[(c, j)] = r[:, 1, :]
 
         def scale_out(c, j):
             j0 = 0
@@ -169,7 +194,7 @@ def tile_attention_pa_kernel(tc, x_bytes, x_scale, Wq, Wk, out_0, out_1):
                 res[(c, j0)] = keep.tile([P, HPG, jw, HD], F32, name="res%d_%d" % (c, j0))
             nc.vector.scalar_tensor_tensor(
                 out=res[(c, j0)][:, :, j - j0, :],
-                in0=rn[(c, j)][:].unsqueeze(2).to_broadcast([P, HPG, HD]),
+                in0=rn[(c, j)].unsqueeze(2).to_broadcast([P, HPG, HD]),
                 scalar=1.0e12,
                 in1=bank[(c, j)][:].rearrange("p (h d) -> p h d", d=HD),
                 op0=ALU.min,
@@ -198,9 +223,13 @@ def tile_attention_pa_kernel(tc, x_bytes, x_scale, Wq, Wk, out_0, out_1):
             if i + 1 < NJ:
                 quant_x(i + 1)
             multiply(c, j)
-            norms(c, j)
-            if i >= 1:
+            if by_vector(c, j):
+                sums_vector(c, j)
                 scale_out(*banks[i - 1])
+            else:
+                sums_scalar(c, j)
+                if i >= 1:
+                    scale_out(*banks[i - 1])
             if i in (1, 2):
                 interleave_w(1, 0, i - 1)
                 interleave_w(1, 1, i - 1)

@@ -27,7 +27,7 @@ HPG = 8
 
 MANUAL = False
 WI_ENGINE = {(0, 0): "s", (0, 1): "v", (1, 0): "s", (1, 1): "v",
-             (2, 0): "g", (2, 1): "g", (3, 0): "g", (3, 1): "g"}
+             (2, 0): "v", (2, 1): "v", (3, 0): "v", (3, 1): "v"}
 WI_PIECES = 2
 STORE_RUNS = {0: (4, 4), 1: (4, 4), 2: (4, 4), 3: (4, 2, 1, 1)}
 V_TILES = (0, 3, 6)
@@ -233,11 +233,8 @@ def tile_attention_pa_kernel(tc, x_bytes, x_scale, Wq, Wk, out_0, out_1):
             if i in (1, 2):
                 interleave_w(1, 0, i - 1)
                 interleave_w(1, 1, i - 1)
-            if i == 7:
-                for cc in (2, 3):
-                    for g in range(NG):
-                        for piece in range(WI_PIECES):
-                            interleave_w(cc, g, piece)
+            if c in (1, 2) and j < NG * WI_PIECES:
+                interleave_w(c + 1, j // WI_PIECES, j % WI_PIECES)
             if c + 1 < NC and j == 4:
                 quant_w(c + 1)
         scale_out(*banks[-1])

@@ -30,7 +30,7 @@ WI_ENGINE = {(0, 0): "s", (0, 1): "v", (1, 0): "s", (1, 1): "v",
              (2, 0): "v", (2, 1): "v", (3, 0): "v", (3, 1): "v"}
 WI_PIECES = 2
 STORE_RUNS = {0: (4, 4), 1: (4, 4), 2: (4, 4), 3: (4, 2, 1, 1)}
-V_TILES = (0, 3, 6)
+V_TILES = ()
 
 
 def by_vector(c, j):

@@ -31,6 +31,7 @@ WI_ENGINE = {(0, 0): "s", (0, 1): "v", (1, 0): "s", (1, 1): "v",
 WI_PIECES = 2
 STORE_RUNS = {0: (4, 4), 1: (4, 4), 2: (4, 4), 3: (4, 2, 1, 1)}
 V_TILES = ()
+RS_AFTER = 2
 
 
 def by_vector(c, j):
@@ -155,7 +156,7 @@ def tile_attention_pa_kernel(tc, x_bytes, x_scale, Wq, Wk, out_0, out_1):
                     stop=(g == NG - 1),
                 )
 
-        stats = {}
+        stats, sums = {}, {}
 
         def sums_vector(c, j):
             acc = bank[(c, j)]
@@ -164,25 +165,21 @@ def tile_attention_pa_kernel(tc, x_bytes, x_scale, Wq, Wk, out_0, out_1):
                 nc.vector.bn_stats(out=st[:, h, :, :].rearrange("p e s -> p (e s)"), in_=acc[:, HD * h:HD * (h + 1)])
             stats[(c, j)] = st
 
-        def sums_scalar(c, j):
+        def rsqrt(c, j):
+            r = small.tile([P, HPG], F32, name="rn")
+            nc.scalar.activation(out=r[:], in_=sums[(c, j)][:], func=ACT.Abs_reciprocal_sqrt)
+            rn[(c, j)] = r[:]
+
+        def sums_scalar(c, j, earlier):
             acc = bank[(c, j)]
-            before = (c, j - 1) if by_vector(c, j - 1) else None
-            ss = small.tile([P, 2, HPG], F32, name="ss")
+            ss = small.tile([P, HPG], F32, name="ss")
+            sums[(c, j)] = ss
             junk = small.tile([P, CW], BF16, name="junk")
             for h in range(HPG):
                 nc.scalar.activation(out=junk[:, HD * h:HD * (h + 1)], in_=acc[:, HD * h:HD * (h + 1)], func=ACT.Square,
-                                     accum_out=ss[:, 1, h:h + 1])
-                if h == 4 and before is not None:
-                    means = stats[before][:, :, :, 1:2]
-                    nc.scalar.activation(out=means, in_=means, func=ACT.Square, scale=math.sqrt(HD / 2))
-            r = small.tile([P, 2, HPG], F32, name="rn")
-            if before is not None:
-                nc.vector.tensor_reduce(out=ss[:, 0, :], in_=stats[before][:, :, :, 1:3], axis=AX.XY, op=ALU.add)
-                nc.scalar.activation(out=r[:], in_=ss[:], func=ACT.Abs_reciprocal_sqrt)
-                rn[before] = r[:, 0, :]
-            else:
-                nc.scalar.activation(out=r[:, 1, :], in_=ss[:, 1, :], func=ACT.Abs_reciprocal_sqrt)
-            rn[(c, j)] = r[:, 1, :]
+                                     accum_out=ss[:, h:h + 1])
+                if h == RS_AFTER and earlier is not None:
+                    rsqrt(*earlier)
 
         def scale_out(c, j):
             j0 = 0
@@ -223,13 +220,9 @@ def tile_attention_pa_kernel(tc, x_bytes, x_scale, Wq, Wk, out_0, out_1):
             if i + 1 < NJ:
                 quant_x(i + 1)
             multiply(c, j)
-            if by_vector(c, j):
-                sums_vector(c, j)
+            sums_scalar(c, j, banks[i - 1] if i >= 1 else None)
+            if i >= 1:
                 scale_out(*banks[i - 1])
-            else:
-                sums_scalar(c, j)
-                if i >= 1:
-                    scale_out(*banks[i - 1])
             if i in (1, 2):
                 interleave_w(1, 0, i - 1)
                 interleave_w(1, 1, i - 1)
@@ -237,4 +230,5 @@ def tile_attention_pa_kernel(tc, x_bytes, x_scale, Wq, Wk, out_0, out_1):
                 interleave_w(c + 1, j // WI_PIECES, j % WI_PIECES)
             if c + 1 < NC and j == 4:
                 quant_w(c + 1)
+        rsqrt(*banks[-1])
         scale_out(*banks[-1])

@@ -1,4 +1,3 @@
-import math
 from contextlib import ExitStack
 
 import concourse.mybir as mybir
@@ -14,10 +13,10 @@ FP8 = mybir.dt.float8_e4m3fn
 FP8X4 = mybir.dt.float8_e4m3fn_x4
 ACT = mybir.ActivationFunctionType
 ALU = mybir.AluOpType
-AX = mybir.AxisListType
 
 P = 128
 NJ = 8
+JH = 4
 K = 1024
 NG = 2
 NC = 4
@@ -30,12 +29,7 @@ WI_ENGINE = {(0, 0): "s", (0, 1): "v", (1, 0): "s", (1, 1): "v",
              (2, 0): "v", (2, 1): "v", (3, 0): "v", (3, 1): "v"}
 WI_PIECES = 2
 STORE_RUNS = {0: (4, 4), 1: (4, 4), 2: (4, 4), 3: (4, 2, 1, 1)}
-V_TILES = ()
 RS_AFTER = 2
-
-
-def by_vector(c, j):
-    return c >= 1 and j in V_TILES
 
 
 def tile_attention_pa_kernel(tc, x_bytes, x_scale, Wq, Wk, out_0, out_1):
@@ -49,9 +43,9 @@ def tile_attention_pa_kernel(tc, x_bytes, x_scale, Wq, Wk, out_0, out_1):
         psum_t = ctx.enter_context(tc.psum_pool(name="psum_t", bufs=2))
         psum_y = ctx.enter_context(tc.psum_pool(name="psum_y", bufs=6))
 
-        xv = x_bytes.rearrange("o (p j) k -> p (o j) k", j=NJ)
+        xv = x_bytes.rearrange("o (a p j) k -> p (o a) j k", p=P, j=JH)
         wviews = [w.rearrange("(g p t) n -> g p t n", g=NG, t=4) for w in (Wq, Wk)]
-        oviews = [o.rearrange("o h (p j) d -> p (o h) j d", j=NJ) for o in (out_0, out_1)]
+        oviews = [o.rearrange("o h (a p j) d -> p (o h) a j d", p=P, j=JH) for o in (out_0, out_1)]
 
         xbytes = [keep.tile([P, 2, K], U8, name="xbytes%d" % i) for i in range(NJ // 2)]
         xs = keep.tile([P, K], F32, name="xs")
@@ -61,7 +55,7 @@ def tile_attention_pa_kernel(tc, x_bytes, x_scale, Wq, Wk, out_0, out_1):
                 wraw[(c, g)] = keep.tile([P, 4, CW], BF16, name="wraw%d_%d" % (c, g))
 
         def load_x(i):
-            nc.sync.dma_start(out=xbytes[i][:], in_=xv[:, 2 * i:2 * i + 2, :])
+            nc.sync.dma_start(out=xbytes[i][:], in_=xv[:, 2 * i // JH, 2 * i % JH:2 * i % JH + 2, :])
 
         def load_w(c, g):
             n0 = (c % 2) * CW
@@ -156,14 +150,7 @@ def tile_attention_pa_kernel(tc, x_bytes, x_scale, Wq, Wk, out_0, out_1):
                     stop=(g == NG - 1),
                 )
 
-        stats, sums = {}, {}
-
-        def sums_vector(c, j):
-            acc = bank[(c, j)]
-            st = small.tile([P, HPG, 2, 3], F32, name="st")
-            for h in range(HPG):
-                nc.vector.bn_stats(out=st[:, h, :, :].rearrange("p e s -> p (e s)"), in_=acc[:, HD * h:HD * (h + 1)])
-            stats[(c, j)] = st
+        sums = {}
 
         def rsqrt(c, j):
             r = small.tile([P, HPG], F32, name="rn")
@@ -199,7 +186,7 @@ def tile_attention_pa_kernel(tc, x_bytes, x_scale, Wq, Wk, out_0, out_1):
             )
             if j == j0 + jw - 1:
                 h0 = (c % 2) * HPG
-                nc.sync.dma_start(out=oviews[c // 2][:, h0:h0 + HPG, j0:j0 + jw, :], in_=res[(c, j0)][:])
+                nc.sync.dma_start(out=oviews[c // 2][:, h0:h0 + HPG, j0 // JH, j0 % JH:j0 % JH + jw, :], in_=res[(c, j0)][:])
 
         product(0)
         turn(0)

@@ -118,8 +118,8 @@ def tile_attention_pa_kernel(tc, x_bytes, x_scale, Wq, Wk, out_0, out_1):
                     wg[c] = keep.tile([P, NG, CW, 4], BF16, name="wg%d" % c, align_bytes=64)
             w = CW // WI_PIECES
             a = piece * w
-            dst = wg[c][:, g, a:a + w, :]
-            src = wraw[(c, g)][:, :, a:a + w].rearrange("p t n -> p n t")
+            dst = wg[c][:, g, a:a + w, :].rearrange("p (b i) t -> p b t i", i=4)
+            src = wraw[(c, g)][:, :, a:a + w].rearrange("p t (b i) -> p b t i", i=4)
             e = WI_ENGINE[(c, g)]
             if e == "v":
                 nc.vector.tensor_copy(out=dst, in_=src)

@@ -24,7 +24,6 @@ CW = 512
 HD = 64
 HPG = 8
 
-MANUAL = False
 WI_ENGINE = {(0, 0): "s", (0, 1): "v", (1, 0): "s", (1, 1): "v",
              (2, 0): "v", (2, 1): "v", (3, 0): "v", (3, 1): "v"}
 WI_PIECES = 2
@@ -35,11 +34,8 @@ RS_AFTER = 2
 def tile_attention_pa_kernel(tc, x_bytes, x_scale, Wq, Wk, out_0, out_1):
     nc = tc.nc
     with ExitStack() as ctx:
-        if MANUAL:
-            ctx.enter_context(tc.manual_schedule())
         keep = ctx.enter_context(tc.tile_pool(name="keep", bufs=1))
         small = ctx.enter_context(tc.tile_pool(name="small", bufs=6))
-        shared = ctx.enter_context(tc.tile_pool(name="shared", bufs=1))
         psum_t = ctx.enter_context(tc.psum_pool(name="psum_t", bufs=2))
         psum_y = ctx.enter_context(tc.psum_pool(name="psum_y", bufs=6))
 
@@ -48,7 +44,7 @@ def tile_attention_pa_kernel(tc, x_bytes, x_scale, Wq, Wk, out_0, out_1):
         oviews = [o.rearrange("o h (a p j) d -> p (o h) a j d", p=P, j=JH) for o in (out_0, out_1)]
 
         xbytes = [keep.tile([P, 2, K], U8, name="xbytes%d" % i) for i in range(NJ // 2)]
-        xs = keep.tile([P, K], F32, name="xs")
+        xs = keep.tile([P, NG, 4], F32, name="xs")
         wraw = {}
         for c in range(NC):
             for g in range(NG):
@@ -61,7 +57,7 @@ def tile_attention_pa_kernel(tc, x_bytes, x_scale, Wq, Wk, out_0, out_1):
             n0 = (c % 2) * CW
             nc.sync.dma_start(out=wraw[(c, g)][:], in_=wviews[c // 2][g, :, :, n0:n0 + CW])
 
-        nc.scalar.dma_start(out=xs[:], in_=x_scale.rearrange("a b k -> (a b k)").partition_broadcast(P))
+        nc.scalar.dma_start(out=xs[:], in_=x_scale.rearrange("a b (g p t) -> p (a b g) t", g=NG, t=4))
         load_x(0)
         load_w(0, 0)
         load_w(0, 1)
@@ -82,25 +78,26 @@ def tile_attention_pa_kernel(tc, x_bytes, x_scale, Wq, Wk, out_0, out_1):
         warm2 = keep.tile([P, 1], F32, name="warm2")
         nc.scalar.activation(out=warm2[:], in_=warm[:], func=ACT.Abs_reciprocal_sqrt)
 
-        xb, xg, xc, xsc = {}, {}, {}, {}
+        xb, pt, xg, xc, xsc = {}, {}, {}, {}, {}
 
-        def product(j):
+        def widen(j):
             xb[j] = keep.tile([P, K], BF16, name="xb%d" % j)
-            nc.vector.tensor_tensor(out=xb[j][:], in0=xbytes[j // 2][:, j % 2, :].bitcast(FP8), in1=xs[:], op=ALU.mult)
+            nc.scalar.copy(out=xb[j][:], in_=xbytes[j // 2][:, j % 2, :].bitcast(FP8))
 
         def turn(j):
             words = xb[j][:].bitcast(F32)
-            pt = psum_t.tile([P, NG, 2, P], F32, name="pt")
+            pt[j] = psum_t.tile([P, 2, NG, P], F32, name="pt")
             for g in range(NG):
                 for u in range(2):
-                    nc.tensor.transpose(pt[:, g, u, :], words[:, 256 * g + u:256 * (g + 1):2], ident[:])
-            if j < 4:
-                xg[j] = keep.tile([P, NG * P * 4], BF16, name="xg%d" % j, align_bytes=64)
-            else:
-                xg[j] = shared.tile([P, NG * P * 4], BF16, name="xg%d" % j, align_bytes=64, offset=(j - 4) * 2048)
-            nc.scalar.copy(
-                out=xg[j][:].bitcast(F32).rearrange("p (g r u) -> p g r u", g=NG, u=2),
-                in_=pt[:].rearrange("p g u r -> p g r u"),
+                    nc.tensor.transpose(pt[j][:, u, g, :], words[:, 256 * g + u:256 * (g + 1):2], ident[:])
+
+        def product(j):
+            xg[j] = keep.tile([P, NG * P * 4], BF16, name="xg%d" % j, align_bytes=64)
+            nc.vector.tensor_tensor(
+                out=xg[j][:].rearrange("p (g r u e) -> p g r u e", g=NG, u=2, e=2),
+                in0=pt[j][:].bitcast(BF16).rearrange("p u g (r e) -> p g r u e", e=2),
+                in1=xs[:].rearrange("p g (u e) -> p g u e", e=2).unsqueeze(2).to_broadcast([P, NG, P, 2, 2]),
+                op=ALU.mult,
             )
 
         def quant_x(j):
@@ -112,10 +109,7 @@ def tile_attention_pa_kernel(tc, x_bytes, x_scale, Wq, Wk, out_0, out_1):
 
         def interleave_w(c, g, piece):
             if c not in wg:
-                if c == 2:
-                    wg[c] = shared.tile([P, NG, CW, 4], BF16, name="wg%d" % c, align_bytes=64, offset=0)
-                else:
-                    wg[c] = keep.tile([P, NG, CW, 4], BF16, name="wg%d" % c, align_bytes=64)
+                wg[c] = keep.tile([P, NG, CW, 4], BF16, name="wg%d" % c, align_bytes=64)
             w = CW // WI_PIECES
             a = piece * w
             dst = wg[c][:, g, a:a + w, :].rearrange("p (b i) t -> p b t i", i=4)
@@ -123,10 +117,8 @@ def tile_attention_pa_kernel(tc, x_bytes, x_scale, Wq, Wk, out_0, out_1):
             e = WI_ENGINE[(c, g)]
             if e == "v":
                 nc.vector.tensor_copy(out=dst, in_=src)
-            elif e == "s":
-                nc.scalar.copy(out=dst, in_=src)
             else:
-                nc.gpsimd.tensor_scalar(out=dst, in0=src, scalar1=1.0, scalar2=0.0, op0=ALU.mult, op1=ALU.add)
+                nc.scalar.copy(out=dst, in_=src)
 
         def quant_w(c):
             wc[c] = keep.tile([P, NG * CW], U32, name="wc%d" % c, align_bytes=64)
@@ -188,22 +180,28 @@ def tile_attention_pa_kernel(tc, x_bytes, x_scale, Wq, Wk, out_0, out_1):
                 h0 = (c % 2) * HPG
                 nc.sync.dma_start(out=oviews[c // 2][:, h0:h0 + HPG, j0 // JH, j0 % JH:j0 % JH + jw, :], in_=res[(c, j0)][:])
 
-        product(0)
+        widen(0)
         turn(0)
-        product(1)
+        widen(1)
         turn(1)
+        product(0)
         for piece in range(WI_PIECES):
             interleave_w(0, 0, piece)
             interleave_w(0, 1, piece)
-        quant_w(0)
         quant_x(0)
-        product(2)
+        product(1)
+        quant_w(0)
+        widen(2)
+        turn(2)
+        widen(3)
         banks = [(c, j) for c in range(NC) for j in range(NJ)]
         for i, (c, j) in enumerate(banks):
+            if i + 4 < NJ:
+                widen(i + 4)
             if i + 3 < NJ:
-                product(i + 3)
+                turn(i + 3)
             if i + 2 < NJ:
-                turn(i + 2)
+                product(i + 2)
             if i + 1 < NJ:
                 quant_x(i + 1)
             multiply(c, j)

@@ -26,7 +26,8 @@ HPG = 8
 
 WI_ENGINE = {(0, 0): "s", (0, 1): "v", (1, 0): "s", (1, 1): "v",
              (2, 0): "v", (2, 1): "v", (3, 0): "v", (3, 1): "v"}
-WI_PIECES = 2
+HALF = 256
+
 STORE_RUNS = {0: (4, 4), 1: (4, 4), 2: (4, 4), 3: (4, 2, 1, 1)}
 RS_AFTER = 2
 
@@ -34,6 +35,7 @@ RS_AFTER = 2
 def tile_attention_pa_kernel(tc, x_bytes, x_scale, Wq, Wk, out_0, out_1):
     nc = tc.nc
     with ExitStack() as ctx:
+        ctx.enter_context(tc.manual_schedule())
         keep = ctx.enter_context(tc.tile_pool(name="keep", bufs=1))
         small = ctx.enter_context(tc.tile_pool(name="small", bufs=6))
         psum_t = ctx.enter_context(tc.psum_pool(name="psum_t", bufs=2))
@@ -107,15 +109,16 @@ def tile_attention_pa_kernel(tc, x_bytes, x_scale, Wq, Wk, out_0, out_1):
 
         wg, wc, wsc = {}, {}, {}
 
-        def interleave_w(c, g, piece):
+        def grouped(c):
             if c not in wg:
                 wg[c] = keep.tile([P, NG, CW, 4], BF16, name="wg%d" % c, align_bytes=64)
-            w = CW // WI_PIECES
-            a = piece * w
-            dst = wg[c][:, g, a:a + w, :].rearrange("p (b i) t -> p b t i", i=4)
-            src = wraw[(c, g)][:, :, a:a + w].rearrange("p t (b i) -> p b t i", i=4)
-            e = WI_ENGINE[(c, g)]
-            if e == "v":
+            return wg[c]
+
+        def interleave_w(c, g, h):
+            n = slice(HALF * h, HALF * (h + 1))
+            dst = grouped(c)[:, g, n, :].rearrange("p (b i) t -> p b t i", i=4)
+            src = wraw[(c, g)][:, :, n].rearrange("p t (b i) -> p b t i", i=4)
+            if WI_ENGINE[(c, g)] == "v":
                 nc.vector.tensor_copy(out=dst, in_=src)
             else:
                 nc.scalar.copy(out=dst, in_=src)
@@ -180,40 +183,42 @@ def tile_attention_pa_kernel(tc, x_bytes, x_scale, Wq, Wk, out_0, out_1):
                 h0 = (c % 2) * HPG
                 nc.sync.dma_start(out=oviews[c // 2][:, h0:h0 + HPG, j0 // JH, j0 % JH:j0 % JH + jw, :], in_=res[(c, j0)][:])
 
+        halves = [(g, h) for g in range(NG) for h in range(2)]
         widen(0)
         turn(0)
+        product(0)
         widen(1)
         turn(1)
-        product(0)
-        for piece in range(WI_PIECES):
-            interleave_w(0, 0, piece)
-            interleave_w(0, 1, piece)
-        quant_x(0)
+        for g, h in halves:
+            interleave_w(0, g, h)
         product(1)
-        quant_w(0)
+        quant_x(0)
         widen(2)
         turn(2)
+        quant_w(0)
+        quant_x(1)
         widen(3)
+        turn(3)
+        product(2)
         banks = [(c, j) for c in range(NC) for j in range(NJ)]
         for i, (c, j) in enumerate(banks):
             if i + 4 < NJ:
                 widen(i + 4)
-            if i + 3 < NJ:
-                turn(i + 3)
-            if i + 2 < NJ:
-                product(i + 2)
-            if i + 1 < NJ:
-                quant_x(i + 1)
             multiply(c, j)
+            if i + 3 < NJ:
+                product(i + 3)
+            if i + 4 < NJ:
+                turn(i + 4)
+            if i + 2 < NJ:
+                quant_x(i + 2)
             sums_scalar(c, j, banks[i - 1] if i >= 1 else None)
             if i >= 1:
                 scale_out(*banks[i - 1])
-            if i in (1, 2):
-                interleave_w(1, 0, i - 1)
-                interleave_w(1, 1, i - 1)
-            if c in (1, 2) and j < NG * WI_PIECES:
-                interleave_w(c + 1, j // WI_PIECES, j % WI_PIECES)
-            if c + 1 < NC and j == 4:
+            if c == 0 and j < 4:
+                interleave_w(1, j % 2, j // 2)
+            if c in (1, 2) and j < 4:
+                interleave_w(c + 1, *halves[j])
+            if j == (NJ - 3 if c == 0 else 4) and c + 1 < NC:
                 quant_w(c + 1)
         rsqrt(*banks[-1])
         scale_out(*banks[-1])

@@ -13,6 +13,7 @@ FP8 = mybir.dt.float8_e4m3fn
 FP8X4 = mybir.dt.float8_e4m3fn_x4
 ACT = mybir.ActivationFunctionType
 ALU = mybir.AluOpType
+AX = mybir.AxisListType
 
 P = 128
 NJ = 8
@@ -24,12 +25,15 @@ CW = 512
 HD = 64
 HPG = 8
 
-WI_ENGINE = {(0, 0): "s", (0, 1): "v", (1, 0): "s", (1, 1): "v",
-             (2, 0): "v", (2, 1): "v", (3, 0): "v", (3, 1): "v"}
+WI = {(0, 0, 0): "s", (0, 0, 1): "s", (1, 0, 0): "s", (1, 0, 1): "s", (1, 1, 0): "s", (1, 1, 1): "s"}
 HALF = 256
 
 STORE_RUNS = {0: (4, 4), 1: (4, 4), 2: (4, 4), 3: (4, 2, 1, 1)}
-RS_AFTER = 2
+WIDE = {(3, 2), (3, 5)}
+LAG_WIDE = 12
+WIDE_WORK = 4
+LAG = 2
+HEAD_PIECES = 2
 
 
 def tile_attention_pa_kernel(tc, x_bytes, x_scale, Wq, Wk, out_0, out_1):
@@ -38,6 +42,7 @@ def tile_attention_pa_kernel(tc, x_bytes, x_scale, Wq, Wk, out_0, out_1):
         ctx.enter_context(tc.manual_schedule())
         keep = ctx.enter_context(tc.tile_pool(name="keep", bufs=1))
         small = ctx.enter_context(tc.tile_pool(name="small", bufs=6))
+        wide = ctx.enter_context(tc.tile_pool(name="wide", bufs=2))
         psum_t = ctx.enter_context(tc.psum_pool(name="psum_t", bufs=2))
         psum_y = ctx.enter_context(tc.psum_pool(name="psum_y", bufs=6))
 
@@ -46,6 +51,10 @@ def tile_attention_pa_kernel(tc, x_bytes, x_scale, Wq, Wk, out_0, out_1):
         oviews = [o.rearrange("o h (a p j) d -> p (o h) a j d", p=P, j=JH) for o in (out_0, out_1)]
 
         xbytes = [keep.tile([P, 2, K], U8, name="xbytes%d" % i) for i in range(NJ // 2)]
+
+        def load_x_tile(j):
+            nc.sync.dma_start(out=xbytes[j // 2][:, j % 2, :], in_=xv[:, j // JH, j % JH, :])
+
         xs = keep.tile([P, NG, 4], F32, name="xs")
         wraw = {}
         for c in range(NC):
@@ -60,8 +69,9 @@ def tile_attention_pa_kernel(tc, x_bytes, x_scale, Wq, Wk, out_0, out_1):
             nc.sync.dma_start(out=wraw[(c, g)][:], in_=wviews[c // 2][g, :, :, n0:n0 + CW])
 
         nc.scalar.dma_start(out=xs[:], in_=x_scale.rearrange("a b (g p t) -> p (a b g) t", g=NG, t=4))
-        load_x(0)
+        load_x_tile(0)
         load_w(0, 0)
+        load_x_tile(1)
         load_w(0, 1)
         load_x(1)
         load_w(1, 0)
@@ -118,7 +128,7 @@ def tile_attention_pa_kernel(tc, x_bytes, x_scale, Wq, Wk, out_0, out_1):
             n = slice(HALF * h, HALF * (h + 1))
             dst = grouped(c)[:, g, n, :].rearrange("p (b i) t -> p b t i", i=4)
             src = wraw[(c, g)][:, :, n].rearrange("p t (b i) -> p b t i", i=4)
-            if WI_ENGINE[(c, g)] == "v":
+            if WI.get((c, g, h), "v") == "v":
                 nc.vector.tensor_copy(out=dst, in_=src)
             else:
                 nc.scalar.copy(out=dst, in_=src)
@@ -129,7 +139,9 @@ def tile_attention_pa_kernel(tc, x_bytes, x_scale, Wq, Wk, out_0, out_1):
             nc.vector.quantize_mx(out=wc[c][:].bitcast(FP8X4), scales=wsc[c][:],
                                   in_=wg[c][:].rearrange("p g n t -> p (g n t)"))
 
-        bank, rn, res = {}, {}, {}
+        banks = [(c, j) for c in range(NC) for j in range(NJ)]
+
+        bank, rn, res, left = {}, {}, {}, {}
 
         def multiply(c, j):
             acc = psum_y.tile([P, CW], F32, name="acc")
@@ -145,25 +157,49 @@ def tile_attention_pa_kernel(tc, x_bytes, x_scale, Wq, Wk, out_0, out_1):
                     stop=(g == NG - 1),
                 )
 
-        sums = {}
+        sums, waiting = {}, []
+        whole = slice(0, HPG)
 
-        def rsqrt(c, j):
-            r = small.tile([P, HPG], F32, name="rn")
-            nc.scalar.activation(out=r[:], in_=sums[(c, j)][:], func=ACT.Abs_reciprocal_sqrt)
-            rn[(c, j)] = r[:]
+        def root(b, heads):
+            if b not in rn:
+                rn[b] = small.tile([P, HPG], F32, name="rn")
+            nc.scalar.activation(out=rn[b][:, heads], in_=sums[b][:, heads], func=ACT.Abs_reciprocal_sqrt)
 
-        def sums_scalar(c, j, earlier):
+        def advance(work):
+            done = []
+            for entry in list(waiting):
+                entry[2] -= work
+                if entry[2] <= 0:
+                    waiting.remove(entry)
+                    root(*entry[:2])
+                    done.append(entry[:2])
+            return done
+
+        def sums_of(i):
+            c, j = banks[i]
             acc = bank[(c, j)]
             ss = small.tile([P, HPG], F32, name="ss")
             sums[(c, j)] = ss
+            ready = []
+            if (c, j) in WIDE:
+                squares = wide.tile([P, CW], F32, name="squares")
+                nc.scalar.activation(out=squares[:], in_=acc[:], func=ACT.Square)
+                nc.vector.tensor_reduce(out=ss[:], in_=squares[:].rearrange("p (h d) -> p h d", d=HD), axis=AX.X, op=ALU.add)
+                ready += advance(WIDE_WORK)
+                waiting.append([banks[i], whole, LAG_WIDE])
+                return ready
             junk = small.tile([P, CW], BF16, name="junk")
             for h in range(HPG):
                 nc.scalar.activation(out=junk[:, HD * h:HD * (h + 1)], in_=acc[:, HD * h:HD * (h + 1)], func=ACT.Square,
                                      accum_out=ss[:, h:h + 1])
-                if h == RS_AFTER and earlier is not None:
-                    rsqrt(*earlier)
+                ready += advance(1)
+                if i == len(banks) - 1 and h == HPG // 2 - 1:
+                    waiting.append([banks[i], slice(0, HPG // 2), LAG])
+            waiting.append([banks[i], slice(HPG // 2, HPG) if i == len(banks) - 1 else whole, LAG])
+            return ready
 
-        def scale_out(c, j):
+        def scale_out(b, heads):
+            c, j = b
             j0 = 0
             for jw in STORE_RUNS[c]:
                 if j < j0 + jw:
@@ -171,17 +207,21 @@ def tile_attention_pa_kernel(tc, x_bytes, x_scale, Wq, Wk, out_0, out_1):
                 j0 += jw
             if (c, j0) not in res:
                 res[(c, j0)] = keep.tile([P, HPG, jw, HD], F32, name="res%d_%d" % (c, j0))
+            n = heads.stop - heads.start
             nc.vector.scalar_tensor_tensor(
-                out=res[(c, j0)][:, :, j - j0, :],
-                in0=rn[(c, j)].unsqueeze(2).to_broadcast([P, HPG, HD]),
+                out=res[(c, j0)][:, heads, j - j0, :],
+                in0=rn[(c, j)][:, heads].unsqueeze(2).to_broadcast([P, n, HD]),
                 scalar=1.0e12,
-                in1=bank[(c, j)][:].rearrange("p (h d) -> p h d", d=HD),
+                in1=bank[(c, j)][:, HD * heads.start:HD * heads.stop].rearrange("p (h d) -> p h d", d=HD),
                 op0=ALU.min,
                 op1=ALU.mult,
             )
-            if j == j0 + jw - 1:
+            left[(c, j0)] = left.get((c, j0), jw * HPG) - n
+            if left[(c, j0)] == 0 or jw == 1:
                 h0 = (c % 2) * HPG
-                nc.sync.dma_start(out=oviews[c // 2][:, h0:h0 + HPG, j0 // JH, j0 % JH:j0 % JH + jw, :], in_=res[(c, j0)][:])
+                part = heads if jw == 1 else slice(0, HPG)
+                nc.sync.dma_start(out=oviews[c // 2][:, h0 + part.start:h0 + part.stop, j0 // JH, j0 % JH:j0 % JH + jw, :],
+                                  in_=res[(c, j0)][:, part])
 
         halves = [(g, h) for g in range(NG) for h in range(2)]
         widen(0)
@@ -200,7 +240,9 @@ def tile_attention_pa_kernel(tc, x_bytes, x_scale, Wq, Wk, out_0, out_1):
         widen(3)
         turn(3)
         product(2)
-        banks = [(c, j) for c in range(NC) for j in range(NJ)]
+        first = [(1, g, h) for h in range(2) for g in range(NG)]
+        for piece in first[:HEAD_PIECES]:
+            interleave_w(*piece)
         for i, (c, j) in enumerate(banks):
             if i + 4 < NJ:
                 widen(i + 4)
@@ -211,14 +253,13 @@ def tile_attention_pa_kernel(tc, x_bytes, x_scale, Wq, Wk, out_0, out_1):
                 turn(i + 4)
             if i + 2 < NJ:
                 quant_x(i + 2)
-            sums_scalar(c, j, banks[i - 1] if i >= 1 else None)
-            if i >= 1:
-                scale_out(*banks[i - 1])
-            if c == 0 and j < 4:
-                interleave_w(1, j % 2, j // 2)
+            for ready in sums_of(i):
+                scale_out(*ready)
+            for piece in first[HEAD_PIECES + i:HEAD_PIECES + i + 1]:
+                interleave_w(*piece)
             if c in (1, 2) and j < 4:
                 interleave_w(c + 1, *halves[j])
-            if j == (NJ - 3 if c == 0 else 4) and c + 1 < NC:
+            if j == (NJ - 3 if c == 0 else 3) and c + 1 < NC:
                 quant_w(c + 1)
-        rsqrt(*banks[-1])
-        scale_out(*banks[-1])
+        for ready in advance(2 * HPG):
+            scale_out(*ready)

@@ -26,14 +26,15 @@ HD = 64
 HPG = 8
 
 WI = {(0, 0, 0): "s", (0, 0, 1): "s", (1, 0, 0): "s", (1, 0, 1): "s", (1, 1, 0): "s", (1, 1, 1): "s"}
+SPREAD = []
 HALF = 256
 
-STORE_RUNS = {0: (4, 4), 1: (4, 4), 2: (4, 4), 3: (4, 2, 1, 1)}
-WIDE = {(3, 2), (3, 5)}
+STORE_RUNS = {0: (4, 4), 1: (4, 4), 2: (4, 4), 3: (2, 2, 2, 2)}
+WIDE = set()
 LAG_WIDE = 12
 WIDE_WORK = 4
+QUANT_AT = (5, 4, 4, 8)
 LAG = 2
-HEAD_PIECES = 2
 
 
 def tile_attention_pa_kernel(tc, x_bytes, x_scale, Wq, Wk, out_0, out_1):
@@ -84,6 +85,8 @@ def tile_attention_pa_kernel(tc, x_bytes, x_scale, Wq, Wk, out_0, out_1):
 
         ident = keep.tile([P, P], F32, name="ident")
         make_identity(nc, ident[:])
+        identb = keep.tile([P, P], BF16, name="identb")
+        nc.vector.tensor_copy(out=identb[:], in_=ident[:])
 
         warm = keep.tile([P, 1], F32, name="warm")
         nc.vector.memset(warm[:], 1.0)
@@ -132,6 +135,30 @@ def tile_attention_pa_kernel(tc, x_bytes, x_scale, Wq, Wk, out_0, out_1):
                 nc.vector.tensor_copy(out=dst, in_=src)
             else:
                 nc.scalar.copy(out=dst, in_=src)
+
+        pw = {}
+
+        def spread_w(c, g, h, q):
+            if q == 0:
+                pw[(c, g, h)] = psum_y.tile([P, HALF * 4], BF16, name="acc")
+            n0 = HALF * h + 128 * q
+            nc.tensor.matmul(pw[(c, g, h)][:, 512 * q:512 * (q + 1)], lhsT=identb[:],
+                             rhs=wraw[(c, g)][:, :, n0:n0 + 128].rearrange("p t n -> p n t"), start=True, stop=True)
+
+        def empty_w(c, g, h):
+            nc.scalar.copy(out=grouped(c)[:, g, HALF * h:HALF * (h + 1), :].rearrange("p n t -> p (n t)").bitcast(F32),
+                           in_=pw[(c, g, h)][:].bitcast(F32))
+
+        def spread_at(i):
+            for half, i0, i1, at_ in SPREAD:
+                for q, at in enumerate((i0, i1)):
+                    if at == i:
+                        spread_w(*half, q)
+
+        def empty_at(i):
+            for half, i0, i1, at in SPREAD:
+                if at == i:
+                    empty_w(*half)
 
         def quant_w(c):
             wc[c] = keep.tile([P, NG * CW], U32, name="wc%d" % c, align_bytes=64)
@@ -217,9 +244,10 @@ def tile_attention_pa_kernel(tc, x_bytes, x_scale, Wq, Wk, out_0, out_1):
                 op1=ALU.mult,
             )
             left[(c, j0)] = left.get((c, j0), jw * HPG) - n
-            if left[(c, j0)] == 0 or jw == 1:
+            last = b == banks[-1]
+            if left[(c, j0)] == 0 or last:
                 h0 = (c % 2) * HPG
-                part = heads if jw == 1 else slice(0, HPG)
+                part = heads if last else whole
                 nc.sync.dma_start(out=oviews[c // 2][:, h0 + part.start:h0 + part.stop, j0 // JH, j0 % JH:j0 % JH + jw, :],
                                   in_=res[(c, j0)][:, part])
 
@@ -235,31 +263,33 @@ def tile_attention_pa_kernel(tc, x_bytes, x_scale, Wq, Wk, out_0, out_1):
         quant_x(0)
         widen(2)
         turn(2)
-        quant_w(0)
-        quant_x(1)
         widen(3)
+        quant_w(0)
+        multiply(*banks[0])
+        quant_x(1)
+        multiply(*banks[1])
         turn(3)
         product(2)
-        first = [(1, g, h) for h in range(2) for g in range(NG)]
-        for piece in first[:HEAD_PIECES]:
-            interleave_w(*piece)
+        interleave_w(1, 0, 0)
         for i, (c, j) in enumerate(banks):
             if i + 4 < NJ:
                 widen(i + 4)
-            multiply(c, j)
             if i + 3 < NJ:
                 product(i + 3)
             if i + 4 < NJ:
                 turn(i + 4)
             if i + 2 < NJ:
                 quant_x(i + 2)
+            spread_at(i)
+            if i + 2 < len(banks):
+                multiply(*banks[i + 2])
             for ready in sums_of(i):
                 scale_out(*ready)
-            for piece in first[HEAD_PIECES + i:HEAD_PIECES + i + 1]:
-                interleave_w(*piece)
+            if c == 0 and 1 <= j < 4:
+                interleave_w(1, *halves[j])
             if c in (1, 2) and j < 4:
                 interleave_w(c + 1, *halves[j])
-            if j == (NJ - 3 if c == 0 else 3) and c + 1 < NC:
+            if j == QUANT_AT[c] and c + 1 < NC:
                 quant_w(c + 1)
         for ready in advance(2 * HPG):
             scale_out(*ready)

@@ -25,14 +25,14 @@ CW = 512
 HD = 64
 HPG = 8
 
-WI = {(0, 0, 0): "s", (0, 0, 1): "s", (1, 0, 0): "s", (1, 0, 1): "s", (1, 1, 0): "s", (1, 1, 1): "s"}
-SPREAD = []
+WI = {(0, 0, 0): "s", (0, 0, 1): "s", (1, 0, 0): "s", (1, 0, 1): "s", (1, 1, 0): "s", (1, 1, 1): "g"}
+PIECES = 4
+XG_AT = 3
 HALF = 256
 
 STORE_RUNS = {0: (4, 4), 1: (4, 4), 2: (4, 4), 3: (2, 2, 2, 2)}
-WIDE = set()
-LAG_WIDE = 12
-WIDE_WORK = 4
+BY_STATS = {(3, 2)}
+LAG_STATS = 10
 QUANT_AT = (5, 4, 4, 8)
 LAG = 2
 
@@ -41,9 +41,9 @@ def tile_attention_pa_kernel(tc, x_bytes, x_scale, Wq, Wk, out_0, out_1):
     nc = tc.nc
     with ExitStack() as ctx:
         ctx.enter_context(tc.manual_schedule())
+        shared = ctx.enter_context(tc.tile_pool(name="shared", bufs=1))
         keep = ctx.enter_context(tc.tile_pool(name="keep", bufs=1))
         small = ctx.enter_context(tc.tile_pool(name="small", bufs=6))
-        wide = ctx.enter_context(tc.tile_pool(name="wide", bufs=2))
         psum_t = ctx.enter_context(tc.psum_pool(name="psum_t", bufs=2))
         psum_y = ctx.enter_context(tc.psum_pool(name="psum_y", bufs=6))
 
@@ -85,8 +85,6 @@ def tile_attention_pa_kernel(tc, x_bytes, x_scale, Wq, Wk, out_0, out_1):
 
         ident = keep.tile([P, P], F32, name="ident")
         make_identity(nc, ident[:])
-        identb = keep.tile([P, P], BF16, name="identb")
-        nc.vector.tensor_copy(out=identb[:], in_=ident[:])
 
         warm = keep.tile([P, 1], F32, name="warm")
         nc.vector.memset(warm[:], 1.0)
@@ -107,7 +105,10 @@ def tile_attention_pa_kernel(tc, x_bytes, x_scale, Wq, Wk, out_0, out_1):
                     nc.tensor.transpose(pt[j][:, u, g, :], words[:, 256 * g + u:256 * (g + 1):2], ident[:])
 
         def product(j):
-            xg[j] = keep.tile([P, NG * P * 4], BF16, name="xg%d" % j, align_bytes=64)
+            if j == 1:
+                xg[j] = shared.tile([P, NG * P * 4], BF16, name="xg%d" % j, align_bytes=64, offset=XG_AT * HALF * 4 * 2)
+            else:
+                xg[j] = keep.tile([P, NG * P * 4], BF16, name="xg%d" % j, align_bytes=64)
             nc.vector.tensor_tensor(
                 out=xg[j][:].rearrange("p (g r u e) -> p g r u e", g=NG, u=2, e=2),
                 in0=pt[j][:].bitcast(BF16).rearrange("p u g (r e) -> p g r u e", e=2),
@@ -123,9 +124,17 @@ def tile_attention_pa_kernel(tc, x_bytes, x_scale, Wq, Wk, out_0, out_1):
         wg, wc, wsc = {}, {}, {}
 
         def grouped(c):
-            if c not in wg:
+            if c not in wg and c > 0:
+                wg[c] = shared.tile([P, NG, CW, 4], BF16, name="wg%d" % c, align_bytes=64, offset=(c - 1) * 3 * HALF * 4 * 2)
+            elif c not in wg:
                 wg[c] = keep.tile([P, NG, CW, 4], BF16, name="wg%d" % c, align_bytes=64)
             return wg[c]
+
+        def interleave_w_gpsimd(c, g, h):
+            w = HALF // PIECES
+            for a in range(HALF * h, HALF * (h + 1), w):
+                nc.gpsimd.tensor_scalar(out=grouped(c)[:, g, a:a + w, :], in0=wraw[(c, g)][:, :, a:a + w].rearrange("p t n -> p n t"),
+                                        scalar1=1.0, scalar2=0.0, op0=ALU.mult, op1=ALU.add)
 
         def interleave_w(c, g, h):
             n = slice(HALF * h, HALF * (h + 1))
@@ -135,30 +144,6 @@ def tile_attention_pa_kernel(tc, x_bytes, x_scale, Wq, Wk, out_0, out_1):
                 nc.vector.tensor_copy(out=dst, in_=src)
             else:
                 nc.scalar.copy(out=dst, in_=src)
-
-        pw = {}
-
-        def spread_w(c, g, h, q):
-            if q == 0:
-                pw[(c, g, h)] = psum_y.tile([P, HALF * 4], BF16, name="acc")
-            n0 = HALF * h + 128 * q
-            nc.tensor.matmul(pw[(c, g, h)][:, 512 * q:512 * (q + 1)], lhsT=identb[:],
-                             rhs=wraw[(c, g)][:, :, n0:n0 + 128].rearrange("p t n -> p n t"), start=True, stop=True)
-
-        def empty_w(c, g, h):
-            nc.scalar.copy(out=grouped(c)[:, g, HALF * h:HALF * (h + 1), :].rearrange("p n t -> p (n t)").bitcast(F32),
-                           in_=pw[(c, g, h)][:].bitcast(F32))
-
-        def spread_at(i):
-            for half, i0, i1, at_ in SPREAD:
-                for q, at in enumerate((i0, i1)):
-                    if at == i:
-                        spread_w(*half, q)
-
-        def empty_at(i):
-            for half, i0, i1, at in SPREAD:
-                if at == i:
-                    empty_w(*half)
 
         def quant_w(c):
             wc[c] = keep.tile([P, NG * CW], U32, name="wc%d" % c, align_bytes=64)
@@ -187,6 +172,19 @@ def tile_attention_pa_kernel(tc, x_bytes, x_scale, Wq, Wk, out_0, out_1):
         sums, waiting = {}, []
         whole = slice(0, HPG)
 
+        stats = {}
+
+        def take_stats(c, j):
+            st = small.tile([P, HPG, 2, 3], F32, name="st")
+            stats[(c, j)] = st
+            for h in range(HPG):
+                nc.vector.bn_stats(out=st[:, h].rearrange("p e v -> p (e v)"), in_=bank[(c, j)][:, HD * h:HD * (h + 1)])
+
+        def sum_stats(b):
+            means = stats[b][:, :, :, 1]
+            nc.vector.scalar_tensor_tensor(out=means, in0=means, scalar=32.0, in1=means, op0=ALU.mult, op1=ALU.mult)
+            nc.vector.tensor_reduce(out=sums[b][:], in_=stats[b][:, :, :, 1:3], axis=AX.XY, op=ALU.add)
+
         def root(b, heads):
             if b not in rn:
                 rn[b] = small.tile([P, HPG], F32, name="rn")
@@ -208,12 +206,8 @@ def tile_attention_pa_kernel(tc, x_bytes, x_scale, Wq, Wk, out_0, out_1):
             ss = small.tile([P, HPG], F32, name="ss")
             sums[(c, j)] = ss
             ready = []
-            if (c, j) in WIDE:
-                squares = wide.tile([P, CW], F32, name="squares")
-                nc.scalar.activation(out=squares[:], in_=acc[:], func=ACT.Square)
-                nc.vector.tensor_reduce(out=ss[:], in_=squares[:].rearrange("p (h d) -> p h d", d=HD), axis=AX.X, op=ALU.add)
-                ready += advance(WIDE_WORK)
-                waiting.append([banks[i], whole, LAG_WIDE])
+            if (c, j) in BY_STATS:
+                waiting.append([banks[i], whole, LAG_STATS])
                 return ready
             junk = small.tile([P, CW], BF16, name="junk")
             for h in range(HPG):
@@ -271,6 +265,7 @@ def tile_attention_pa_kernel(tc, x_bytes, x_scale, Wq, Wk, out_0, out_1):
         turn(3)
         product(2)
         interleave_w(1, 0, 0)
+        interleave_w_gpsimd(1, 1, 1)
         for i, (c, j) in enumerate(banks):
             if i + 4 < NJ:
                 widen(i + 4)
@@ -280,16 +275,22 @@ def tile_attention_pa_kernel(tc, x_bytes, x_scale, Wq, Wk, out_0, out_1):
                 turn(i + 4)
             if i + 2 < NJ:
                 quant_x(i + 2)
-            spread_at(i)
             if i + 2 < len(banks):
                 multiply(*banks[i + 2])
+            if banks[i] in BY_STATS:
+                take_stats(c, j)
             for ready in sums_of(i):
                 scale_out(*ready)
-            if c == 0 and 1 <= j < 4:
+            if banks[i] in BY_STATS:
+                sum_stats(banks[i])
+            if c == 0 and 1 <= j < 3:
                 interleave_w(1, *halves[j])
-            if c in (1, 2) and j < 4:
+            if c in (1, 2) and 1 <= j < 4:
                 interleave_w(c + 1, *halves[j])
             if j == QUANT_AT[c] and c + 1 < NC:
                 quant_w(c + 1)
-        for ready in advance(2 * HPG):
-            scale_out(*ready)
+                if c < 2:
+                    interleave_w_gpsimd(c + 2, 0, 0)
+        while waiting:
+            for ready in advance(2 * HPG):
+                scale_out(*ready)

@@ -25,12 +25,12 @@ CW = 512
 HD = 64
 HPG = 8
 
-WI = {(0, 0, 0): "s", (0, 0, 1): "s", (1, 0, 0): "s", (1, 0, 1): "s", (1, 1, 0): "s", (1, 1, 1): "g"}
+WI = {(0, 0, 1): "s", (0, 1, 0): "s", (1, 0, 0): "s", (1, 0, 1): "s", (1, 1, 0): "s", (1, 1, 1): "g"}
 PIECES = 4
 XG_AT = 3
 HALF = 256
 
-STORE_RUNS = {0: (4, 4), 1: (4, 4), 2: (4, 4), 3: (2, 2, 2, 2)}
+STORE_RUNS = {0: (4, 4), 1: (4, 4), 2: (4, 2, 2), 3: (2, 2, 2, 2)}
 BY_STATS = {(3, 2)}
 LAG_STATS = 10
 QUANT_AT = (5, 4, 4, 8)
@@ -248,26 +248,27 @@ def tile_attention_pa_kernel(tc, x_bytes, x_scale, Wq, Wk, out_0, out_1):
         halves = [(g, h) for g in range(NG) for h in range(2)]
         widen(0)
         turn(0)
+        interleave_w(0, 0, 0)
         product(0)
         widen(1)
         turn(1)
-        for g, h in halves:
+        for g, h in halves[1:]:
             interleave_w(0, g, h)
         product(1)
         quant_x(0)
         widen(2)
         turn(2)
         widen(3)
+        turn(3)
         quant_w(0)
         multiply(*banks[0])
         quant_x(1)
-        multiply(*banks[1])
-        turn(3)
         product(2)
+        widen(4)
         interleave_w(1, 0, 0)
         interleave_w_gpsimd(1, 1, 1)
         for i, (c, j) in enumerate(banks):
-            if i + 4 < NJ:
+            if 4 < i + 4 < NJ:
                 widen(i + 4)
             if i + 3 < NJ:
                 product(i + 3)
@@ -275,6 +276,8 @@ def tile_attention_pa_kernel(tc, x_bytes, x_scale, Wq, Wk, out_0, out_1):
                 turn(i + 4)
             if i + 2 < NJ:
                 quant_x(i + 2)
+            if i == 0:
+                multiply(*banks[1])
             if i + 2 < len(banks):
                 multiply(*banks[i + 2])
             if banks[i] in BY_STATS:
@@ -283,8 +286,10 @@ def tile_attention_pa_kernel(tc, x_bytes, x_scale, Wq, Wk, out_0, out_1):
                 scale_out(*ready)
             if banks[i] in BY_STATS:
                 sum_stats(banks[i])
-            if c == 0 and 1 <= j < 3:
-                interleave_w(1, *halves[j])
+            if c == 0 and j == 2:
+                interleave_w(1, 0, 1)
+            if c == 0 and j == 4:
+                interleave_w(1, 1, 0)
             if c in (1, 2) and 1 <= j < 4:
                 interleave_w(c + 1, *halves[j])
             if j == QUANT_AT[c] and c + 1 < NC:

from contextlib import ExitStack

import concourse.mybir as mybir
from concourse.masks import make_identity

FLOPS = 2 * 1024 * 1024 * 2048

F32 = mybir.dt.float32
BF16 = mybir.dt.bfloat16
U8 = mybir.dt.uint8
U32 = mybir.dt.uint32
FP8 = mybir.dt.float8_e4m3fn
FP8X4 = mybir.dt.float8_e4m3fn_x4
ACT = mybir.ActivationFunctionType
ALU = mybir.AluOpType
AX = mybir.AxisListType

P = 128
NJ = 8
JH = 4
K = 1024
NG = 2
NC = 4
CW = 512
HD = 64
HPG = 8

WI = {(0, 0, 1): "s", (0, 1, 0): "s", (1, 0, 0): "s", (1, 0, 1): "s", (1, 1, 0): "s", (1, 1, 1): "g"}
PIECES = 4
XG_AT = 3
HALF = 256

STORE_RUNS = {0: (4, 4), 1: (4, 4), 2: (4, 2, 2), 3: (2, 2, 2, 2)}
BY_STATS = {(3, 2)}
LAG_STATS = 10
QUANT_AT = (5, 4, 4, 8)
LAG = 2


def tile_attention_pa_kernel(tc, x_bytes, x_scale, Wq, Wk, out_0, out_1):
    nc = tc.nc
    with ExitStack() as ctx:
        ctx.enter_context(tc.manual_schedule())
        shared = ctx.enter_context(tc.tile_pool(name="shared", bufs=1))
        keep = ctx.enter_context(tc.tile_pool(name="keep", bufs=1))
        small = ctx.enter_context(tc.tile_pool(name="small", bufs=6))
        psum_t = ctx.enter_context(tc.psum_pool(name="psum_t", bufs=2))
        psum_y = ctx.enter_context(tc.psum_pool(name="psum_y", bufs=6))

        xv = x_bytes.rearrange("o (a p j) k -> p (o a) j k", p=P, j=JH)
        wviews = [w.rearrange("(g p t) n -> g p t n", g=NG, t=4) for w in (Wq, Wk)]
        oviews = [o.rearrange("o h (a p j) d -> p (o h) a j d", p=P, j=JH) for o in (out_0, out_1)]

        xbytes = [keep.tile([P, 2, K], U8, name="xbytes%d" % i) for i in range(NJ // 2)]

        def load_x_tile(j):
            nc.sync.dma_start(out=xbytes[j // 2][:, j % 2, :], in_=xv[:, j // JH, j % JH, :])

        xs = keep.tile([P, NG, 4], F32, name="xs")
        wraw = {}
        for c in range(NC):
            for g in range(NG):
                wraw[(c, g)] = keep.tile([P, 4, CW], BF16, name="wraw%d_%d" % (c, g))

        def load_x(i):
            nc.sync.dma_start(out=xbytes[i][:], in_=xv[:, 2 * i // JH, 2 * i % JH:2 * i % JH + 2, :])

        def load_w(c, g):
            n0 = (c % 2) * CW
            nc.sync.dma_start(out=wraw[(c, g)][:], in_=wviews[c // 2][g, :, :, n0:n0 + CW])

        nc.scalar.dma_start(out=xs[:], in_=x_scale.rearrange("a b (g p t) -> p (a b g) t", g=NG, t=4))
        load_x_tile(0)
        load_w(0, 0)
        load_x_tile(1)
        load_w(0, 1)
        load_x(1)
        load_w(1, 0)
        load_w(1, 1)
        load_x(2)
        load_x(3)
        for c in range(2, NC):
            for g in range(NG):
                load_w(c, g)

        ident = keep.tile([P, P], F32, name="ident")
        make_identity(nc, ident[:])

        warm = keep.tile([P, 1], F32, name="warm")
        nc.vector.memset(warm[:], 1.0)
        warm2 = keep.tile([P, 1], F32, name="warm2")
        nc.scalar.activation(out=warm2[:], in_=warm[:], func=ACT.Abs_reciprocal_sqrt)

        xb, pt, xg, xc, xsc = {}, {}, {}, {}, {}

        def widen(j):
            xb[j] = keep.tile([P, K], BF16, name="xb%d" % j)
            nc.scalar.copy(out=xb[j][:], in_=xbytes[j // 2][:, j % 2, :].bitcast(FP8))

        def turn(j):
            words = xb[j][:].bitcast(F32)
            pt[j] = psum_t.tile([P, 2, NG, P], F32, name="pt")
            for g in range(NG):
                for u in range(2):
                    nc.tensor.transpose(pt[j][:, u, g, :], words[:, 256 * g + u:256 * (g + 1):2], ident[:])

        def product(j):
            if j == 1:
                xg[j] = shared.tile([P, NG * P * 4], BF16, name="xg%d" % j, align_bytes=64, offset=XG_AT * HALF * 4 * 2)
            else:
                xg[j] = keep.tile([P, NG * P * 4], BF16, name="xg%d" % j, align_bytes=64)
            nc.vector.tensor_tensor(
                out=xg[j][:].rearrange("p (g r u e) -> p g r u e", g=NG, u=2, e=2),
                in0=pt[j][:].bitcast(BF16).rearrange("p u g (r e) -> p g r u e", e=2),
                in1=xs[:].rearrange("p g (u e) -> p g u e", e=2).unsqueeze(2).to_broadcast([P, NG, P, 2, 2]),
                op=ALU.mult,
            )

        def quant_x(j):
            xc[j] = keep.tile([P, NG * P], U32, name="xc%d" % j, align_bytes=64)
            xsc[j] = keep.tile([P, NG * P], U8, name="xsc%d" % j, align_bytes=64)
            nc.vector.quantize_mx(out=xc[j][:].bitcast(FP8X4), scales=xsc[j][:], in_=xg[j][:])

        wg, wc, wsc = {}, {}, {}

        def grouped(c):
            if c not in wg and c > 0:
                wg[c] = shared.tile([P, NG, CW, 4], BF16, name="wg%d" % c, align_bytes=64, offset=(c - 1) * 3 * HALF * 4 * 2)
            elif c not in wg:
                wg[c] = keep.tile([P, NG, CW, 4], BF16, name="wg%d" % c, align_bytes=64)
            return wg[c]

        def interleave_w_gpsimd(c, g, h):
            w = HALF // PIECES
            for a in range(HALF * h, HALF * (h + 1), w):
                nc.gpsimd.tensor_scalar(out=grouped(c)[:, g, a:a + w, :], in0=wraw[(c, g)][:, :, a:a + w].rearrange("p t n -> p n t"),
                                        scalar1=1.0, scalar2=0.0, op0=ALU.mult, op1=ALU.add)

        def interleave_w(c, g, h):
            n = slice(HALF * h, HALF * (h + 1))
            dst = grouped(c)[:, g, n, :].rearrange("p (b i) t -> p b t i", i=4)
            src = wraw[(c, g)][:, :, n].rearrange("p t (b i) -> p b t i", i=4)
            if WI.get((c, g, h), "v") == "v":
                nc.vector.tensor_copy(out=dst, in_=src)
            else:
                nc.scalar.copy(out=dst, in_=src)

        def quant_w(c):
            wc[c] = keep.tile([P, NG * CW], U32, name="wc%d" % c, align_bytes=64)
            wsc[c] = keep.tile([P, NG * CW], U8, name="wsc%d" % c, align_bytes=64)
            nc.vector.quantize_mx(out=wc[c][:].bitcast(FP8X4), scales=wsc[c][:],
                                  in_=wg[c][:].rearrange("p g n t -> p (g n t)"))

        banks = [(c, j) for c in range(NC) for j in range(NJ)]

        bank, rn, res, left = {}, {}, {}, {}

        def multiply(c, j):
            acc = psum_y.tile([P, CW], F32, name="acc")
            bank[(c, j)] = acc
            for g in range(NG):
                nc.tensor.matmul_mx(
                    out=acc[:],
                    lhsT=xc[j][:, P * g:P * (g + 1)].bitcast(FP8X4),
                    lhsT_scale=xsc[j][:, P * g:P * (g + 1)],
                    rhs=wc[c][:, CW * g:CW * (g + 1)].bitcast(FP8X4),
                    rhs_scale=wsc[c][:, CW * g:CW * (g + 1)],
                    start=(g == 0),
                    stop=(g == NG - 1),
                )

        sums, waiting = {}, []
        whole = slice(0, HPG)

        stats = {}

        def take_stats(c, j):
            st = small.tile([P, HPG, 2, 3], F32, name="st")
            stats[(c, j)] = st
            for h in range(HPG):
                nc.vector.bn_stats(out=st[:, h].rearrange("p e v -> p (e v)"), in_=bank[(c, j)][:, HD * h:HD * (h + 1)])

        def sum_stats(b):
            means = stats[b][:, :, :, 1]
            nc.vector.scalar_tensor_tensor(out=means, in0=means, scalar=32.0, in1=means, op0=ALU.mult, op1=ALU.mult)
            nc.vector.tensor_reduce(out=sums[b][:], in_=stats[b][:, :, :, 1:3], axis=AX.XY, op=ALU.add)

        def root(b, heads):
            if b not in rn:
                rn[b] = small.tile([P, HPG], F32, name="rn")
            nc.scalar.activation(out=rn[b][:, heads], in_=sums[b][:, heads], func=ACT.Abs_reciprocal_sqrt)

        def advance(work):
            done = []
            for entry in list(waiting):
                entry[2] -= work
                if entry[2] <= 0:
                    waiting.remove(entry)
                    root(*entry[:2])
                    done.append(entry[:2])
            return done

        def sums_of(i):
            c, j = banks[i]
            acc = bank[(c, j)]
            ss = small.tile([P, HPG], F32, name="ss")
            sums[(c, j)] = ss
            ready = []
            if (c, j) in BY_STATS:
                waiting.append([banks[i], whole, LAG_STATS])
                return ready
            junk = small.tile([P, CW], BF16, name="junk")
            for h in range(HPG):
                nc.scalar.activation(out=junk[:, HD * h:HD * (h + 1)], in_=acc[:, HD * h:HD * (h + 1)], func=ACT.Square,
                                     accum_out=ss[:, h:h + 1])
                ready += advance(1)
                if i == len(banks) - 1 and h == HPG // 2 - 1:
                    waiting.append([banks[i], slice(0, HPG // 2), LAG])
            waiting.append([banks[i], slice(HPG // 2, HPG) if i == len(banks) - 1 else whole, LAG])
            return ready

        def scale_out(b, heads):
            c, j = b
            j0 = 0
            for jw in STORE_RUNS[c]:
                if j < j0 + jw:
                    break
                j0 += jw
            if (c, j0) not in res:
                res[(c, j0)] = keep.tile([P, HPG, jw, HD], F32, name="res%d_%d" % (c, j0))
            n = heads.stop - heads.start
            nc.vector.scalar_tensor_tensor(
                out=res[(c, j0)][:, heads, j - j0, :],
                in0=rn[(c, j)][:, heads].unsqueeze(2).to_broadcast([P, n, HD]),
                scalar=1.0e12,
                in1=bank[(c, j)][:, HD * heads.start:HD * heads.stop].rearrange("p (h d) -> p h d", d=HD),
                op0=ALU.min,
                op1=ALU.mult,
            )
            left[(c, j0)] = left.get((c, j0), jw * HPG) - n
            last = b == banks[-1]
            if left[(c, j0)] == 0 or last:
                h0 = (c % 2) * HPG
                part = heads if last else whole
                nc.sync.dma_start(out=oviews[c // 2][:, h0 + part.start:h0 + part.stop, j0 // JH, j0 % JH:j0 % JH + jw, :],
                                  in_=res[(c, j0)][:, part])

        halves = [(g, h) for g in range(NG) for h in range(2)]
        widen(0)
        turn(0)
        interleave_w(0, 0, 0)
        product(0)
        widen(1)
        turn(1)
        for g, h in halves[1:]:
            interleave_w(0, g, h)
        product(1)
        quant_x(0)
        widen(2)
        turn(2)
        widen(3)
        turn(3)
        quant_w(0)
        multiply(*banks[0])
        quant_x(1)
        product(2)
        widen(4)
        interleave_w(1, 0, 0)
        interleave_w_gpsimd(1, 1, 1)
        for i, (c, j) in enumerate(banks):
            if 4 < i + 4 < NJ:
                widen(i + 4)
            if i + 3 < NJ:
                product(i + 3)
            if i + 4 < NJ:
                turn(i + 4)
            if i + 2 < NJ:
                quant_x(i + 2)
            if i == 0:
                multiply(*banks[1])
            if i + 2 < len(banks):
                multiply(*banks[i + 2])
            if banks[i] in BY_STATS:
                take_stats(c, j)
            for ready in sums_of(i):
                scale_out(*ready)
            if banks[i] in BY_STATS:
                sum_stats(banks[i])
            if c == 0 and j == 2:
                interleave_w(1, 0, 1)
            if c == 0 and j == 4:
                interleave_w(1, 1, 0)
            if c in (1, 2) and 1 <= j < 4:
                interleave_w(c + 1, *halves[j])
            if j == QUANT_AT[c] and c + 1 < NC:
                quant_w(c + 1)
                if c < 2:
                    interleave_w_gpsimd(c + 2, 0, 0)
        while waiting:
            for ready in advance(2 * HPG):
                scale_out(*ready)
